import numpy as np
import ml_dtypes


def mxq(x, axis, fmt="e4m3"):
    dtype, down = {"e4m3": (ml_dtypes.float8_e4m3fn, 7), "e5m2": (ml_dtypes.float8_e5m2, 14)}[fmt]
    v = np.moveaxis(np.asarray(x, np.float32).astype(ml_dtypes.bfloat16).astype(np.float64), axis, -1)
    blocks = v.reshape(v.shape[:-1] + (-1, 32))
    amax = np.abs(blocks).max(-1, keepdims=True)
    byte = np.maximum(np.where(amax > 0, np.frexp(amax)[1] - 1 + 127, 0) - down, 1)
    scale = np.exp2(byte - 127.0)
    codes = (blocks / scale).astype(np.float32).astype(dtype).astype(np.float64)
    return np.moveaxis((codes * scale).reshape(v.shape), -1, axis)


WIDE = False


def mx_kscale(k):
    if not WIDE:
        return np.ones(k)
    levels = np.array([10, -10, 5, -5, 0])
    if k % 512:
        return np.exp2(np.random.permutation(np.resize(levels, k // 32))).repeat(32)
    a = np.empty((k // 512, 16))
    for p in range(k // 512):
        a[p, :8] = np.random.permutation(np.resize(levels, 8))
        for g in range(8):
            far = levels[np.abs(levels - a[p, g]) >= 10]
            a[p, g + 8] = far[np.random.randint(len(far))]
    return np.exp2(a.ravel()).repeat(32)


BF16 = ml_dtypes.bfloat16


def bf(x):
    return np.asarray(x, np.float32).astype(BF16)


def f64(x):
    return np.asarray(x).astype(np.float64)


B, C, K, H, W = 2, 512, 64, 128, 128
N = H * W


def setup_inputs():
    s = mx_kscale(N)
    feats = np.random.standard_normal((B, C, N)) * 4.0 * s.mean() / s
    probs = np.random.standard_normal((B, K, N)) * 2.0 + np.log(s)
    return {"feats": bf(feats.reshape(B, C, H, W)), "probs": bf(probs.reshape(B, K, H, W))}


def reference(feats, probs):
    x = f64(feats).reshape(B, C, N)
    l = f64(probs).reshape(B, K, N)
    e = np.exp(l - l.max(2, keepdims=True))
    ctx = (mxq(e, 2, "e4m3") @ mxq(x, 2, "e4m3").transpose(0, 2, 1)) / e.sum(2, keepdims=True)
    return ctx.transpose(0, 2, 1)[..., None]

@@ -1,0 +1,289 @@
+from contextlib import ExitStack
+
+import concourse.mybir as mybir
+from concourse.masks import make_identity
+
+F32 = mybir.dt.float32
+BF16 = mybir.dt.bfloat16
+U32 = mybir.dt.uint32
+U8 = mybir.dt.uint8
+I32 = mybir.dt.int32
+FP8X4 = mybir.dt.float8_e4m3fn_x4
+ALU = mybir.AluOpType
+ACT = mybir.ActivationFunctionType
+AX = mybir.AxisListType
+
+P = 128
+B, C, K, N = 2, 512, 64, 16384
+FLOPS = 2 * B * K * C * N
+
+NP = N // 512
+PROB_CHUNKS = (2048, 2048, 2048, 2048, 2048, 2048, 2048, 1024, 1024)
+CHUNKS = (1, 1, 2, 4, 4, 4, 4, 4, 4, 2, 1, 1)
+XBUFS = {1: 4, 2: 2, 4: 5}
+ESTEP = 192
+ER = 8
+EXP_OFF = -2
+ET_OFF = -1
+EC_OFF = 0
+EQ_OFF = 0
+Q_OFF = 1
+MX_OFF = 3
+XGB = 3
+XCB = 4
+EARLY = 0
+WARM = ()
+VSKIP = 8
+
+
+def tile_spatialgather_module_kernel(tc, feats, probs, out):
+    nc = tc.nc
+    x = feats.rearrange("b c h w -> b c (h w)")
+    l = probs.rearrange("b k h w -> (b k) (h w)")
+    o = out.rearrange("b (t p) k o -> p (b t) (k o)", p=P)
+
+    with ExitStack() as ctx:
+        const = ctx.enter_context(tc.tile_pool(name="const", bufs=1))
+        xsp = ctx.enter_context(tc.tile_pool(name="xsp", bufs=1))
+        xgp = ctx.enter_context(tc.tile_pool(name="xgp", bufs=XGB))
+        xcp = ctx.enter_context(tc.tile_pool(name="xcp", bufs=XCB))
+        jkp = ctx.enter_context(tc.tile_pool(name="jkp", bufs=2))
+        enp = ctx.enter_context(tc.tile_pool(name="enp", bufs=4))
+        egp = ctx.enter_context(tc.tile_pool(name="egp", bufs=3))
+        accp = ctx.enter_context(tc.psum_pool(name="accp", bufs=1))
+        tps = ctx.enter_context(tc.psum_pool(name="tps", bufs=4))
+        tpv = ctx.enter_context(tc.psum_pool(name="tpv", bufs=2))
+        tpe = ctx.enter_context(tc.psum_pool(name="tpe", bufs=1))
+        ctx.enter_context(tc.manual_schedule())
+
+        ident_f = const.tile([P, P], F32, name="ident_f")
+        ident_b = const.tile([P, P], BF16, name="ident_b")
+        perm_b = const.tile([P, P], BF16, name="perm_b")
+        l_sb = const.tile([P, N], BF16, name="l_sb")
+        e_codes = const.tile([P, ER * ESTEP + 64], U32, name="e_codes", align_bytes=64)
+        e_sc = const.tile([P, ER * ESTEP + 64], U8, name="e_sc", align_bytes=64)
+        mcol = const.tile([P, 16], F32, name="mcol")
+        mall = const.tile([P, 1], F32, name="mall")
+        negmax = const.tile([P, 1], F32, name="negmax")
+        rs = const.tile([P, NP], F32, name="rs")
+        rtot = const.tile([P, 1], F32, name="rtot")
+        rinv = const.tile([P, 1], F32, name="rinv")
+        scr0 = const.tile([P, 1], F32, name="scr0")
+        scr1 = const.tile([P, 1], F32, name="scr1")
+        ctx_sb = const.tile([P, C], F32, name="ctx_sb")
+        o_sb = const.tile([P, C], F32, name="o_sb")
+        acc = accp.tile([P, C], F32, name="acc")
+
+        xs_tiles = {}
+        xt_tiles = {}
+        xg_tiles = {}
+        xc_tiles = {}
+        en_tiles = {}
+        et_tiles = {}
+        eg_tiles = {}
+
+        tiles = []
+        units = []
+        g0 = 0
+        for ng in CHUNKS:
+            for b in range(B):
+                for q in range(ng):
+                    units.append((len(tiles), q, b, g0 + q))
+                tiles.append((b, g0, ng))
+            g0 += ng
+
+        def load_x(tau):
+            b, g0, ng = tiles[tau]
+            xs = xsp.tile([P, 4 * 512 * ng], BF16, name="xs%d" % ng, tag="xs%d" % ng, bufs=XBUFS[ng])
+            nc.sync.dma_start(
+                out=xs[:].rearrange("p (c n) -> p c n", c=4),
+                in_=x[b, :, g0 * 512 : (g0 + ng) * 512].rearrange("(c p) n -> p c n", p=P),
+            )
+            xs_tiles[tau] = xs
+
+        def on_vector(st, i, a):
+            return i == 1 and a == 1 and not (VSKIP and st % VSKIP == VSKIP - 1)
+
+        def x_transposes(st, i, a):
+            tau, q = units[2 * st + i][0], units[2 * st + i][1]
+            row = 256 * tiles[tau][2]
+            xw = xs_tiles[tau][:].bitcast(F32)
+            if on_vector(st, i, a):
+                xt = tpv.tile([P, 4, P], F32, name="xtv", tag="xtv")
+            else:
+                xt = tps.tile([P, 4, P], F32, name="xts", tag="xts")
+            for aa in range(2):
+                for u in range(2):
+                    w0 = (2 * a + aa) * row + q * 256
+                    nc.tensor.transpose(xt[:, 2 * aa + u, :], xw[:, w0 + u : w0 + 256 : 2], ident_f[:])
+            xt_tiles[(st, i, a)] = xt
+
+        def x_copy(st, i, a):
+            xt = xt_tiles[(st, i, a)]
+            if i == 0 and a == 0:
+                xg = xgp.tile([P, 4096], BF16, name="xg", tag="xg", align_bytes=64)
+                xg_tiles[st] = xg
+            xg = xg_tiles[st]
+            h0 = (2 * i + a) * 1024
+            dst = xg[:, h0 : h0 + 1024].bitcast(F32).rearrange("p (a c u) -> p a c u", a=2, u=2)
+            src = xt[:].rearrange("p (a u) c -> p a c u", u=2)
+            if on_vector(st, i, a):
+                nc.vector.tensor_copy(out=dst, in_=src)
+            else:
+                nc.scalar.copy(out=dst, in_=src)
+
+        def x_quant(st):
+            xc = xcp.tile([P, 2 * C], U32, name="xc", tag="xc", align_bytes=64)
+            xsc = xcp.tile([P, 2 * C], U8, name="xsc", tag="xsc", align_bytes=64)
+            xc_tiles[st] = (xc, xsc)
+            nc.vector.quantize_mx(out=xc[:].bitcast(FP8X4), scales=xsc[:], in_=xg_tiles[st][:])
+
+        def mx_pass(st, i):
+            b, g = units[2 * st + i][2], units[2 * st + i][3]
+            xc, xsc = xc_tiles[st]
+            w0 = (g % ER) * ESTEP + (1 - b) * P
+            nc.tensor.matmul_mx(
+                out=acc[:],
+                lhsT=e_codes[:, w0 : w0 + P].bitcast(FP8X4),
+                lhsT_scale=e_sc[:, w0 : w0 + P],
+                rhs=xc[:, i * C : (i + 1) * C].bitcast(FP8X4),
+                rhs_scale=xsc[:, i * C : (i + 1) * C],
+                start=(len(WARM) == 0 and st == 0 and i == 0),
+                stop=(st == NP - 1 and i == 1),
+            )
+
+        def e_exp(g):
+            en = enp.tile([P, 512], BF16, name="en", tag="en")
+            nc.scalar.activation(
+                out=en[:],
+                in_=l_sb[:, g * 512 : (g + 1) * 512],
+                func=ACT.Exp,
+                bias=negmax[:, 0:1],
+                scale=1.0,
+                accum_out=rs[:, g : g + 1],
+            )
+            en_tiles[g] = en
+
+        def e_transposes(g):
+            v = en_tiles[g][:].rearrange("p (q u e) -> p u e q", u=2, e=2)
+            et = tpe.tile([P, 4, P], BF16, name="et", tag="et")
+            for u in range(2):
+                for e in range(2):
+                    nc.tensor.transpose(et[:, 2 * u + e, :], v[:, u, e, :], perm_b[:])
+            et_tiles[g] = et
+
+        def e_copy(g):
+            eg = egp.tile([P, 512], BF16, name="eg", tag="eg", align_bytes=64)
+            nc.vector.tensor_copy(
+                out=eg[:].rearrange("p (r t) -> p r t", t=4), in_=et_tiles[g][:].rearrange("p t r -> p r t")
+            )
+            eg_tiles[g] = eg
+
+        def e_quant(g):
+            w0 = (g % ER) * ESTEP + 64
+            nc.vector.quantize_mx(
+                out=e_codes[:, w0 : w0 + P].bitcast(FP8X4), scales=e_sc[:, w0 : w0 + P], in_=eg_tiles[g][:]
+            )
+
+        off = 0
+        for w in PROB_CHUNKS:
+            nc.sync.dma_start(out=l_sb[:, off : off + w], in_=l[:, off : off + w])
+            off += w
+        holder = []
+        for tau in range(len(tiles)):
+            same = [t for t in range(tau) if tiles[t][2] == tiles[tau][2]]
+            nb = XBUFS[tiles[tau][2]]
+            holder.append(same[-nb] if len(same) >= nb else -1)
+        loaded = [0]
+
+        def load_more(done):
+            while loaded[0] < len(tiles) and holder[loaded[0]] <= done:
+                load_x(loaded[0])
+                loaded[0] += 1
+
+        load_more(-1)
+
+        make_identity(nc, ident_f[:])
+        make_identity(nc, ident_b[:])
+        nc.gpsimd.tensor_copy(out=perm_b[:, 0:64], in_=ident_b[:, 64:128])
+        nc.gpsimd.tensor_copy(out=perm_b[:, 64:128], in_=ident_b[:, 0:64])
+        nc.vector.memset(scr0[:], 0.0)
+        nc.vector.memset(e_codes[:].bitcast(I32), 0)
+        nc.vector.memset(e_sc[:].bitcast(I32), 0)
+        nc.scalar.activation(out=scr1[:], in_=scr0[:], func=ACT.Exp)
+
+        off = 0
+        for i, w in enumerate(PROB_CHUNKS):
+            junk = jkp.tile([P, w], BF16, name="junk", tag="junk")
+            nc.vector.tensor_scalar(
+                out=junk[:],
+                in0=l_sb[:, off : off + w],
+                scalar1=0.0,
+                scalar2=None,
+                op0=ALU.add,
+                op1=ALU.max,
+                accum_out=mcol[:, i : i + 1],
+            )
+            off += w
+        nc.vector.tensor_reduce(out=mall[:], in_=mcol[:, 0 : len(PROB_CHUNKS)], axis=AX.X, op=ALU.max)
+        nc.vector.tensor_scalar(out=negmax[:], in0=mall[:], scalar1=-1.0, scalar2=None, op0=ALU.mult)
+
+        def e_work(st, off, fn):
+            if 0 <= st - off < NP:
+                fn(st - off)
+
+        for st in range(EXP_OFF, NP + MX_OFF):
+            if 0 <= st - 1 < NP and on_vector(st - 1, 1, 1):
+                x_copy(st - 1, 1, 1)
+            if 0 <= st < NP:
+                for i in range(2):
+                    for a in range(2):
+                        x_transposes(st, i, a)
+                for i in range(2):
+                    for a in range(2):
+                        if not on_vector(st, i, a):
+                            x_copy(st, i, a)
+            e_work(st, EXP_OFF, e_exp)
+            if st == 0:
+                for g in range(-ET_OFF):
+                    e_transposes(g)
+            e_work(st, EC_OFF, e_copy)
+            if 0 <= st - Q_OFF < NP:
+                x_quant(st - Q_OFF)
+            e_work(st, EQ_OFF, e_quant)
+            if st >= 0:
+                e_work(st, ET_OFF, e_transposes)
+            if 0 <= st - MX_OFF < NP:
+                for i in range(2):
+                    mx_pass(st - MX_OFF, i)
+            if 0 <= st < NP:
+                for i in range(2):
+                    tau, q = units[2 * st + i][0], units[2 * st + i][1]
+                    if q == tiles[tau][2] - 1:
+                        load_more(tau)
+            if st == NP:
+                nc.vector.tensor_reduce(out=rtot[:], in_=rs[:], axis=AX.X, op=ALU.add)
+                nc.vector.reciprocal(out=rinv[:], in_=rtot[:])
+
+        o_v = o_sb[:].rearrange("p (b t k) -> p b t k", b=B, k=K)
+        for a in range(2):
+            nc.vector.tensor_scalar(
+                out=ctx_sb[:, a * 256 : (a + 1) * 256],
+                in0=acc[:, a * 256 : (a + 1) * 256],
+                scalar1=rinv[:, 0:1],
+                scalar2=None,
+                op0=ALU.mult,
+            )
+            if a == 0:
+                ot = tpv.tile([P, 2, P], F32, name="otv", tag="xtv")
+            else:
+                ot = tps.tile([P, 2, P], F32, name="ots", tag="xts")
+            for i in range(2):
+                t = 2 * a + i
+                nc.tensor.transpose(ot[:, i, :], ctx_sb[:, t * P : (t + 1) * P], ident_f[:])
+            src = ot[:].rearrange("p t (b k) -> p b t k", b=B)
+            if a == 0:
+                nc.scalar.copy(out=o_v[:, :, 0:2, :], in_=src)
+            else:
+                nc.vector.tensor_copy(out=o_v[:, :, 2:4, :], in_=src)
+        nc.sync.dma_start(out=o, in_=o_sb[:].rearrange("p (g k) -> p g k", k=K))

@@ -19,21 +19,13 @@ FLOPS = 2 * B * K * C * N
 
 NP = N // 512
 PROB_CHUNKS = (2048, 2048, 2048, 2048, 2048, 2048, 2048, 1024, 1024)
-CHUNKS = (1, 1, 2, 4, 4, 4, 4, 4, 4, 2, 1, 1)
-XBUFS = {1: 4, 2: 2, 4: 5}
+CHUNKS = (1, 1) + (2,) * 14 + (1, 1)
+XBUFS = {1: 2, 2: 6}
 ESTEP = 192
 ER = 8
-EXP_OFF = -2
-ET_OFF = -1
-EC_OFF = 0
-EQ_OFF = 0
-Q_OFF = 1
-MX_OFF = 3
 XGB = 3
 XCB = 4
-EARLY = 0
-WARM = ()
-VSKIP = 8
+PREPARED = tuple(range(5, NP, 2))
 
 
 def tile_spatialgather_module_kernel(tc, feats, probs, out):
@@ -45,6 +37,7 @@ def tile_spatialgather_module_kernel(tc, feats, probs, out):
     with ExitStack() as ctx:
         const = ctx.enter_context(tc.tile_pool(name="const", bufs=1))
         xsp = ctx.enter_context(tc.tile_pool(name="xsp", bufs=1))
+        xdp = ctx.enter_context(tc.tile_pool(name="xdp", bufs=2))
         xgp = ctx.enter_context(tc.tile_pool(name="xgp", bufs=XGB))
         xcp = ctx.enter_context(tc.tile_pool(name="xcp", bufs=XCB))
         jkp = ctx.enter_context(tc.tile_pool(name="jkp", bufs=2))
@@ -57,8 +50,7 @@ def tile_spatialgather_module_kernel(tc, feats, probs, out):
         ctx.enter_context(tc.manual_schedule())
 
         ident_f = const.tile([P, P], F32, name="ident_f")
-        ident_b = const.tile([P, P], BF16, name="ident_b")
-        perm_b = const.tile([P, P], BF16, name="perm_b")
+        perm_f = const.tile([P, P], F32, name="perm_f")
         l_sb = const.tile([P, N], BF16, name="l_sb")
         e_codes = const.tile([P, ER * ESTEP + 64], U32, name="e_codes", align_bytes=64)
         e_sc = const.tile([P, ER * ESTEP + 64], U8, name="e_sc", align_bytes=64)
@@ -75,6 +67,7 @@ def tile_spatialgather_module_kernel(tc, feats, probs, out):
         acc = accp.tile([P, C], F32, name="acc")
 
         xs_tiles = {}
+        xd_tiles = {}
         xt_tiles = {}
         xg_tiles = {}
         xc_tiles = {}
@@ -82,41 +75,55 @@ def tile_spatialgather_module_kernel(tc, feats, probs, out):
         et_tiles = {}
         eg_tiles = {}
 
-        tiles = []
-        units = []
-        g0 = 0
-        for ng in CHUNKS:
-            for b in range(B):
-                for q in range(ng):
-                    units.append((len(tiles), q, b, g0 + q))
-                tiles.append((b, g0, ng))
-            g0 += ng
+        chunk_of = []
+        first_pass = []
+        for tau, ng in enumerate(CHUNKS):
+            first_pass.append(len(chunk_of))
+            for q in range(ng):
+                chunk_of.append((tau, q))
 
         def load_x(tau):
-            b, g0, ng = tiles[tau]
-            xs = xsp.tile([P, 4 * 512 * ng], BF16, name="xs%d" % ng, tag="xs%d" % ng, bufs=XBUFS[ng])
-            nc.sync.dma_start(
-                out=xs[:].rearrange("p (c n) -> p c n", c=4),
-                in_=x[b, :, g0 * 512 : (g0 + ng) * 512].rearrange("(c p) n -> p c n", p=P),
-            )
+            ng, g0 = CHUNKS[tau], first_pass[tau]
+            xs = xsp.tile([P, 8 * 512 * ng], BF16, name="xs%d" % ng, tag="xs%d" % ng, bufs=XBUFS[ng])
+            for b in range(B):
+                nc.sync.dma_start(
+                    out=xs[:, b * 2048 * ng : (b + 1) * 2048 * ng].rearrange("p (c n) -> p c n", c=4),
+                    in_=x[b, :, g0 * 512 : (g0 + ng) * 512].rearrange("(c p) n -> p c n", p=P),
+                )
             xs_tiles[tau] = xs
 
-        def on_vector(st, i, a):
-            return i == 1 and a == 1 and not (VSKIP and st % VSKIP == VSKIP - 1)
+        def x_prepare(g, b):
+            tau, q = chunk_of[g]
+            ng = CHUNKS[tau]
+            if b == 0:
+                xd_tiles[g] = xdp.tile([P, 4096], BF16, name="xd", tag="xd")
+            src = xs_tiles[tau][:, b * 2048 * ng : (b + 1) * 2048 * ng].rearrange("p (c n) -> p c n", c=4)
+            src = src[:, :, q * 512 : (q + 1) * 512].rearrange("p c (j u i) -> p u c j i", u=2, i=16)
+            dst = xd_tiles[g][:, b * 2048 : (b + 1) * 2048].rearrange("p (u c j i) -> p u c j i", u=2, c=4, i=16)
+            for u in range(2):
+                nc.vector.tensor_copy(out=dst[:, u, :, :, :], in_=src[:, u, :, :, :])
 
-        def x_transposes(st, i, a):
-            tau, q = units[2 * st + i][0], units[2 * st + i][1]
-            row = 256 * tiles[tau][2]
-            xw = xs_tiles[tau][:].bitcast(F32)
-            if on_vector(st, i, a):
+        def on_vector(st, i, a):
+            return i == 1 and a == 1 and st % 2 == 0
+
+        def x_transposes(g, b, a):
+            tau, q = chunk_of[g]
+            row = 256 * CHUNKS[tau]
+            if on_vector(g, b, a):
                 xt = tpv.tile([P, 4, P], F32, name="xtv", tag="xtv")
             else:
                 xt = tps.tile([P, 4, P], F32, name="xts", tag="xts")
             for aa in range(2):
+                c = 2 * a + aa
                 for u in range(2):
-                    w0 = (2 * a + aa) * row + q * 256
-                    nc.tensor.transpose(xt[:, 2 * aa + u, :], xw[:, w0 + u : w0 + 256 : 2], ident_f[:])
-            xt_tiles[(st, i, a)] = xt
+                    if g in PREPARED:
+                        w0 = b * 1024 + u * 512 + c * P
+                        src = xd_tiles[g][:].bitcast(F32)[:, w0 : w0 + P]
+                    else:
+                        w0 = (4 * b + c) * row + q * 256
+                        src = xs_tiles[tau][:].bitcast(F32)[:, w0 + u : w0 + 256 : 2]
+                    nc.tensor.transpose(xt[:, 2 * aa + u, :], src, ident_f[:])
+            xt_tiles[(g, b, a)] = xt
 
         def x_copy(st, i, a):
             xt = xt_tiles[(st, i, a)]
@@ -138,44 +145,43 @@ def tile_spatialgather_module_kernel(tc, feats, probs, out):
             xc_tiles[st] = (xc, xsc)
             nc.vector.quantize_mx(out=xc[:].bitcast(FP8X4), scales=xsc[:], in_=xg_tiles[st][:])
 
-        def mx_pass(st, i):
-            b, g = units[2 * st + i][2], units[2 * st + i][3]
-            xc, xsc = xc_tiles[st]
+        def mx_pass(g, b):
+            xc, xsc = xc_tiles[g]
             w0 = (g % ER) * ESTEP + (1 - b) * P
             nc.tensor.matmul_mx(
                 out=acc[:],
                 lhsT=e_codes[:, w0 : w0 + P].bitcast(FP8X4),
                 lhsT_scale=e_sc[:, w0 : w0 + P],
-                rhs=xc[:, i * C : (i + 1) * C].bitcast(FP8X4),
-                rhs_scale=xsc[:, i * C : (i + 1) * C],
-                start=(len(WARM) == 0 and st == 0 and i == 0),
-                stop=(st == NP - 1 and i == 1),
+                rhs=xc[:, b * C : (b + 1) * C].bitcast(FP8X4),
+                rhs_scale=xsc[:, b * C : (b + 1) * C],
+                start=(g == 0 and b == 0),
+                stop=(g == NP - 1 and b == 1),
             )
 
         def e_exp(g):
             en = enp.tile([P, 512], BF16, name="en", tag="en")
+            dst = en[:]
+            src = l_sb[:, g * 512 : (g + 1) * 512]
+            if g in PREPARED:
+                dst = dst.rearrange("p (u j i) -> p j u i", u=2, i=16)
+                src = src.rearrange("p (j u i) -> p j u i", u=2, i=16)
             nc.scalar.activation(
-                out=en[:],
-                in_=l_sb[:, g * 512 : (g + 1) * 512],
-                func=ACT.Exp,
-                bias=negmax[:, 0:1],
-                scale=1.0,
-                accum_out=rs[:, g : g + 1],
+                out=dst, in_=src, func=ACT.Exp, bias=negmax[:, 0:1], scale=1.0, accum_out=rs[:, g : g + 1]
             )
             en_tiles[g] = en
 
         def e_transposes(g):
-            v = en_tiles[g][:].rearrange("p (q u e) -> p u e q", u=2, e=2)
-            et = tpe.tile([P, 4, P], BF16, name="et", tag="et")
+            ew = en_tiles[g][:].bitcast(F32)
+            et = tpe.tile([P, 2, P], F32, name="et", tag="et")
             for u in range(2):
-                for e in range(2):
-                    nc.tensor.transpose(et[:, 2 * u + e, :], v[:, u, e, :], perm_b[:])
+                src = ew[:, u * P : (u + 1) * P] if g in PREPARED else ew[:, u:256:2]
+                nc.tensor.transpose(et[:, u, :], src, perm_f[:])
             et_tiles[g] = et
 
         def e_copy(g):
             eg = egp.tile([P, 512], BF16, name="eg", tag="eg", align_bytes=64)
             nc.vector.tensor_copy(
-                out=eg[:].rearrange("p (r t) -> p r t", t=4), in_=et_tiles[g][:].rearrange("p t r -> p r t")
+                out=eg[:].bitcast(F32).rearrange("p (r u) -> p r u", u=2), in_=et_tiles[g][:].rearrange("p u r -> p r u")
             )
             eg_tiles[g] = eg
 
@@ -190,23 +196,22 @@ def tile_spatialgather_module_kernel(tc, feats, probs, out):
             nc.sync.dma_start(out=l_sb[:, off : off + w], in_=l[:, off : off + w])
             off += w
         holder = []
-        for tau in range(len(tiles)):
-            same = [t for t in range(tau) if tiles[t][2] == tiles[tau][2]]
-            nb = XBUFS[tiles[tau][2]]
+        for tau in range(len(CHUNKS)):
+            same = [t for t in range(tau) if CHUNKS[t] == CHUNKS[tau]]
+            nb = XBUFS[CHUNKS[tau]]
             holder.append(same[-nb] if len(same) >= nb else -1)
         loaded = [0]
 
         def load_more(done):
-            while loaded[0] < len(tiles) and holder[loaded[0]] <= done:
+            while loaded[0] < len(CHUNKS) and holder[loaded[0]] <= done:
                 load_x(loaded[0])
                 loaded[0] += 1
 
         load_more(-1)
 
         make_identity(nc, ident_f[:])
-        make_identity(nc, ident_b[:])
-        nc.gpsimd.tensor_copy(out=perm_b[:, 0:64], in_=ident_b[:, 64:128])
-        nc.gpsimd.tensor_copy(out=perm_b[:, 64:128], in_=ident_b[:, 0:64])
+        nc.gpsimd.tensor_copy(out=perm_f[:, 0:64], in_=ident_f[:, 64:128])
+        nc.gpsimd.tensor_copy(out=perm_f[:, 64:128], in_=ident_f[:, 0:64])
         nc.vector.memset(scr0[:], 0.0)
         nc.vector.memset(e_codes[:].bitcast(I32), 0)
         nc.vector.memset(e_sc[:].bitcast(I32), 0)
@@ -228,39 +233,38 @@ def tile_spatialgather_module_kernel(tc, feats, probs, out):
         nc.vector.tensor_reduce(out=mall[:], in_=mcol[:, 0 : len(PROB_CHUNKS)], axis=AX.X, op=ALU.max)
         nc.vector.tensor_scalar(out=negmax[:], in0=mall[:], scalar1=-1.0, scalar2=None, op0=ALU.mult)
 
-        def e_work(st, off, fn):
-            if 0 <= st - off < NP:
-                fn(st - off)
-
-        for st in range(EXP_OFF, NP + MX_OFF):
+        for st in range(-2, NP + 3):
             if 0 <= st - 1 < NP and on_vector(st - 1, 1, 1):
                 x_copy(st - 1, 1, 1)
             if 0 <= st < NP:
-                for i in range(2):
+                for b in range(B):
                     for a in range(2):
-                        x_transposes(st, i, a)
-                for i in range(2):
+                        x_transposes(st, b, a)
+                for b in range(B):
                     for a in range(2):
-                        if not on_vector(st, i, a):
-                            x_copy(st, i, a)
-            e_work(st, EXP_OFF, e_exp)
+                        if not on_vector(st, b, a):
+                            x_copy(st, b, a)
+            if 0 <= st + 2 < NP:
+                e_exp(st + 2)
             if st == 0:
-                for g in range(-ET_OFF):
-                    e_transposes(g)
-            e_work(st, EC_OFF, e_copy)
-            if 0 <= st - Q_OFF < NP:
-                x_quant(st - Q_OFF)
-            e_work(st, EQ_OFF, e_quant)
-            if st >= 0:
-                e_work(st, ET_OFF, e_transposes)
-            if 0 <= st - MX_OFF < NP:
-                for i in range(2):
-                    mx_pass(st - MX_OFF, i)
+                e_transposes(0)
             if 0 <= st < NP:
-                for i in range(2):
-                    tau, q = units[2 * st + i][0], units[2 * st + i][1]
-                    if q == tiles[tau][2] - 1:
-                        load_more(tau)
+                e_copy(st)
+            if st >= 0 and st + 2 in PREPARED:
+                x_prepare(st + 2, 1)
+            if 0 <= st - 1 < NP:
+                x_quant(st - 1)
+            if 0 <= st < NP:
+                e_quant(st)
+            if st >= 0 and st + 3 in PREPARED:
+                x_prepare(st + 3, 0)
+            if 0 <= st and st + 1 < NP:
+                e_transposes(st + 1)
+            if 0 <= st - 3 < NP:
+                for b in range(B):
+                    mx_pass(st - 3, b)
+            if 0 <= st < NP and chunk_of[st][1] == CHUNKS[chunk_of[st][0]] - 1:
+                load_more(chunk_of[st][0])
             if st == NP:
                 nc.vector.tensor_reduce(out=rtot[:], in_=rs[:], axis=AX.X, op=ALU.add)
                 nc.vector.reciprocal(out=rinv[:], in_=rtot[:])

@@ -25,7 +25,7 @@ ESTEP = 192
 ER = 8
 XGB = 3
 XCB = 4
-PREPARED = tuple(range(5, NP, 2))
+FIRST_SORTED = 3
 
 
 def tile_spatialgather_module_kernel(tc, feats, probs, out):
@@ -92,16 +92,14 @@ def tile_spatialgather_module_kernel(tc, feats, probs, out):
                 )
             xs_tiles[tau] = xs
 
-        def x_prepare(g, b):
+        def x_prepare(g):
             tau, q = chunk_of[g]
-            ng = CHUNKS[tau]
-            if b == 0:
-                xd_tiles[g] = xdp.tile([P, 4096], BF16, name="xd", tag="xd")
-            src = xs_tiles[tau][:, b * 2048 * ng : (b + 1) * 2048 * ng].rearrange("p (c n) -> p c n", c=4)
-            src = src[:, :, q * 512 : (q + 1) * 512].rearrange("p c (j u i) -> p u c j i", u=2, i=16)
-            dst = xd_tiles[g][:, b * 2048 : (b + 1) * 2048].rearrange("p (u c j i) -> p u c j i", u=2, c=4, i=16)
-            for u in range(2):
-                nc.vector.tensor_copy(out=dst[:, u, :, :, :], in_=src[:, u, :, :, :])
+            row = 256 * CHUNKS[tau]
+            xd_tiles[g] = xdp.tile([P, 1024], F32, name="xd", tag="xd")
+            src = xs_tiles[tau][:].bitcast(F32)[:, 0 : 4 * row].rearrange("p (c n) -> p c n", c=4)
+            src = src[:, :, q * 256 : (q + 1) * 256].rearrange("p c (w u) -> p u c w", u=2)
+            dst = xd_tiles[g][:].rearrange("p (u c w) -> p u c w", u=2, c=4)
+            nc.vector.tensor_copy(out=dst, in_=src)
 
         def on_vector(st, i, a):
             return i == 1 and a == 1 and st % 2 == 0
@@ -116,9 +114,9 @@ def tile_spatialgather_module_kernel(tc, feats, probs, out):
             for aa in range(2):
                 c = 2 * a + aa
                 for u in range(2):
-                    if g in PREPARED:
-                        w0 = b * 1024 + u * 512 + c * P
-                        src = xd_tiles[g][:].bitcast(F32)[:, w0 : w0 + P]
+                    if b == 0 and g >= FIRST_SORTED:
+                        w0 = u * 512 + c * P
+                        src = xd_tiles[g][:, w0 : w0 + P]
                     else:
                         w0 = (4 * b + c) * row + q * 256
                         src = xs_tiles[tau][:].bitcast(F32)[:, w0 + u : w0 + 256 : 2]
@@ -160,11 +158,8 @@ def tile_spatialgather_module_kernel(tc, feats, probs, out):
 
         def e_exp(g):
             en = enp.tile([P, 512], BF16, name="en", tag="en")
-            dst = en[:]
-            src = l_sb[:, g * 512 : (g + 1) * 512]
-            if g in PREPARED:
-                dst = dst.rearrange("p (u j i) -> p j u i", u=2, i=16)
-                src = src.rearrange("p (j u i) -> p j u i", u=2, i=16)
+            dst = en[:].rearrange("p (u w e) -> p u w e", u=2, e=2)
+            src = l_sb[:, g * 512 : (g + 1) * 512].rearrange("p (w u e) -> p u w e", u=2, e=2)
             nc.scalar.activation(
                 out=dst, in_=src, func=ACT.Exp, bias=negmax[:, 0:1], scale=1.0, accum_out=rs[:, g : g + 1]
             )
@@ -174,8 +169,7 @@ def tile_spatialgather_module_kernel(tc, feats, probs, out):
             ew = en_tiles[g][:].bitcast(F32)
             et = tpe.tile([P, 2, P], F32, name="et", tag="et")
             for u in range(2):
-                src = ew[:, u * P : (u + 1) * P] if g in PREPARED else ew[:, u:256:2]
-                nc.tensor.transpose(et[:, u, :], src, perm_f[:])
+                nc.tensor.transpose(et[:, u, :], ew[:, u * P : (u + 1) * P], perm_f[:])
             et_tiles[g] = et
 
         def e_copy(g):
@@ -250,14 +244,12 @@ def tile_spatialgather_module_kernel(tc, feats, probs, out):
                 e_transposes(0)
             if 0 <= st < NP:
                 e_copy(st)
-            if st >= 0 and st + 2 in PREPARED:
-                x_prepare(st + 2, 1)
             if 0 <= st - 1 < NP:
                 x_quant(st - 1)
             if 0 <= st < NP:
                 e_quant(st)
-            if st >= 0 and st + 3 in PREPARED:
-                x_prepare(st + 3, 0)
+            if FIRST_SORTED <= st + 2 < NP and st >= 0:
+                x_prepare(st + 2)
             if 0 <= st and st + 1 < NP:
                 e_transposes(st + 1)
             if 0 <= st - 3 < NP:

@@ -57,7 +57,7 @@ def tile_spatialgather_module_kernel(tc, feats, probs, out):
         mcol = const.tile([P, 16], F32, name="mcol")
         mall = const.tile([P, 1], F32, name="mall")
         negmax = const.tile([P, 1], F32, name="negmax")
-        rs = const.tile([P, NP], F32, name="rs")
+        rs = const.tile([P, NP // 2], F32, name="rs")
         rtot = const.tile([P, 1], F32, name="rtot")
         rinv = const.tile([P, 1], F32, name="rinv")
         scr0 = const.tile([P, 1], F32, name="scr0")
@@ -102,7 +102,9 @@ def tile_spatialgather_module_kernel(tc, feats, probs, out):
             nc.vector.tensor_copy(out=dst, in_=src)
 
         def on_vector(st, i, a):
-            return i == 1 and a == 1 and st % 2 == 0
+            if st == NP - 1:
+                return i == 1
+            return i == 1 and a == 1 and st % 2 == 1
 
         def x_transposes(g, b, a):
             tau, q = chunk_of[g]
@@ -141,7 +143,9 @@ def tile_spatialgather_module_kernel(tc, feats, probs, out):
             xc = xcp.tile([P, 2 * C], U32, name="xc", tag="xc", align_bytes=64)
             xsc = xcp.tile([P, 2 * C], U8, name="xsc", tag="xsc", align_bytes=64)
             xc_tiles[st] = (xc, xsc)
-            nc.vector.quantize_mx(out=xc[:].bitcast(FP8X4), scales=xsc[:], in_=xg_tiles[st][:])
+            for b in range(B) if st == NP - 1 else [0]:
+                w = C if st == NP - 1 else 2 * C
+                nc.vector.quantize_mx(out=xc[:, b * C : b * C + w].bitcast(FP8X4), scales=xsc[:, b * C : b * C + w], in_=xg_tiles[st][:, 4 * b * C : 4 * b * C + 4 * w])
 
         def mx_pass(g, b):
             xc, xsc = xc_tiles[g]
@@ -157,19 +161,19 @@ def tile_spatialgather_module_kernel(tc, feats, probs, out):
             )
 
         def e_exp(g):
-            en = enp.tile([P, 512], BF16, name="en", tag="en")
+            en = enp.tile([P, 1024], BF16, name="en", tag="en")
             dst = en[:].rearrange("p (u w e) -> p u w e", u=2, e=2)
-            src = l_sb[:, g * 512 : (g + 1) * 512].rearrange("p (w u e) -> p u w e", u=2, e=2)
+            src = l_sb[:, g * 512 : (g + 2) * 512].rearrange("p (w u e) -> p u w e", u=2, e=2)
             nc.scalar.activation(
-                out=dst, in_=src, func=ACT.Exp, bias=negmax[:, 0:1], scale=1.0, accum_out=rs[:, g : g + 1]
+                out=dst, in_=src, func=ACT.Exp, bias=negmax[:, 0:1], scale=1.0, accum_out=rs[:, g // 2 : g // 2 + 1]
             )
-            en_tiles[g] = en
+            en_tiles[g] = en_tiles[g + 1] = en
 
         def e_transposes(g):
             ew = en_tiles[g][:].bitcast(F32)
             et = tpe.tile([P, 2, P], F32, name="et", tag="et")
             for u in range(2):
-                nc.tensor.transpose(et[:, u, :], ew[:, u * P : (u + 1) * P], perm_f[:])
+                nc.tensor.transpose(et[:, u, :], ew[:, u * 256 + g % 2 * P : u * 256 + g % 2 * P + P], perm_f[:])
             et_tiles[g] = et
 
         def e_copy(g):
@@ -228,8 +232,9 @@ def tile_spatialgather_module_kernel(tc, feats, probs, out):
         nc.vector.tensor_scalar(out=negmax[:], in0=mall[:], scalar1=-1.0, scalar2=None, op0=ALU.mult)
 
         for st in range(-2, NP + 3):
-            if 0 <= st - 1 < NP and on_vector(st - 1, 1, 1):
-                x_copy(st - 1, 1, 1)
+            for a in range(2):
+                if 0 <= st - 1 < NP and on_vector(st - 1, 1, a):
+                    x_copy(st - 1, 1, a)
             if 0 <= st < NP:
                 for b in range(B):
                     for a in range(2):
@@ -238,7 +243,7 @@ def tile_spatialgather_module_kernel(tc, feats, probs, out):
                     for a in range(2):
                         if not on_vector(st, b, a):
                             x_copy(st, b, a)
-            if 0 <= st + 2 < NP:
+            if 0 <= st + 2 < NP and st % 2 == 0:
                 e_exp(st + 2)
             if st == 0:
                 e_transposes(0)

@@ -18,31 +18,33 @@ B, C, K, N = 2, 512, 64, 16384
 FLOPS = 2 * B * K * C * N
 
 NP = N // 512
+NS = NP
 PROB_CHUNKS = (2048, 2048, 2048, 2048, 2048, 2048, 2048, 1024, 1024)
-CHUNKS = (1, 1) + (2,) * 14 + (1, 1)
-XBUFS = {1: 2, 2: 6}
+XB = 13
+SPLIT_LOADS = 8
 ESTEP = 192
 ER = 8
 XGB = 3
 XCB = 4
-FIRST_SORTED = 3
+SORTED = 2
+FIRST_SORTED = 4
 
 
 def tile_spatialgather_module_kernel(tc, feats, probs, out):
     nc = tc.nc
     x = feats.rearrange("b c h w -> b c (h w)")
     l = probs.rearrange("b k h w -> (b k) (h w)")
-    o = out.rearrange("b (t p) k o -> p (b t) (k o)", p=P)
+    o = out.rearrange("b (t p) k o -> p b t (k o)", p=P)
 
     with ExitStack() as ctx:
         const = ctx.enter_context(tc.tile_pool(name="const", bufs=1))
-        xsp = ctx.enter_context(tc.tile_pool(name="xsp", bufs=1))
+        xsp = ctx.enter_context(tc.tile_pool(name="xsp", bufs=XB))
         xdp = ctx.enter_context(tc.tile_pool(name="xdp", bufs=2))
         xgp = ctx.enter_context(tc.tile_pool(name="xgp", bufs=XGB))
         xcp = ctx.enter_context(tc.tile_pool(name="xcp", bufs=XCB))
         jkp = ctx.enter_context(tc.tile_pool(name="jkp", bufs=2))
-        enp = ctx.enter_context(tc.tile_pool(name="enp", bufs=4))
-        egp = ctx.enter_context(tc.tile_pool(name="egp", bufs=3))
+        enp = ctx.enter_context(tc.tile_pool(name="enp", bufs=3))
+        egp = ctx.enter_context(tc.tile_pool(name="egp", bufs=2))
         accp = ctx.enter_context(tc.psum_pool(name="accp", bufs=1))
         tps = ctx.enter_context(tc.psum_pool(name="tps", bufs=4))
         tpv = ctx.enter_context(tc.psum_pool(name="tpv", bufs=2))
@@ -75,66 +77,55 @@ def tile_spatialgather_module_kernel(tc, feats, probs, out):
         et_tiles = {}
         eg_tiles = {}
 
-        chunk_of = []
-        first_pass = []
-        for tau, ng in enumerate(CHUNKS):
-            first_pass.append(len(chunk_of))
-            for q in range(ng):
-                chunk_of.append((tau, q))
+        def load_x(st):
+            m, b = st // 2, st % 2
+            xs = xsp.tile([P, 4096], BF16, name="xs", tag="xs")
+            dst = xs[:].rearrange("p (c n) -> p c n", c=4)
+            src = x[b, :, m * 1024 : (m + 1) * 1024].rearrange("(c p) n -> p c n", p=P)
+            w = 2 if st < SPLIT_LOADS else 4
+            for c in range(0, 4, w):
+                nc.sync.dma_start(out=dst[:, c : c + w, :], in_=src[:, c : c + w, :])
+            xs_tiles[st] = xs
 
-        def load_x(tau):
-            ng, g0 = CHUNKS[tau], first_pass[tau]
-            xs = xsp.tile([P, 8 * 512 * ng], BF16, name="xs%d" % ng, tag="xs%d" % ng, bufs=XBUFS[ng])
-            for b in range(B):
-                nc.sync.dma_start(
-                    out=xs[:, b * 2048 * ng : (b + 1) * 2048 * ng].rearrange("p (c n) -> p c n", c=4),
-                    in_=x[b, :, g0 * 512 : (g0 + ng) * 512].rearrange("(c p) n -> p c n", p=P),
-                )
-            xs_tiles[tau] = xs
+        def x_prepare(st):
+            xd = xdp.tile([P, 512 * SORTED], F32, name="xd", tag="xd")
+            src = xs_tiles[st][:].bitcast(F32)[:, 0 : 512 * SORTED]
+            nc.vector.tensor_copy(
+                out=xd[:].rearrange("p (u c w) -> p u c w", u=2, c=SORTED),
+                in_=src.rearrange("p (c w u) -> p u c w", c=SORTED, u=2),
+            )
+            xd_tiles[st] = xd
 
-        def x_prepare(g):
-            tau, q = chunk_of[g]
-            row = 256 * CHUNKS[tau]
-            xd_tiles[g] = xdp.tile([P, 1024], F32, name="xd", tag="xd")
-            src = xs_tiles[tau][:].bitcast(F32)[:, 0 : 4 * row].rearrange("p (c n) -> p c n", c=4)
-            src = src[:, :, q * 256 : (q + 1) * 256].rearrange("p c (w u) -> p u c w", u=2)
-            dst = xd_tiles[g][:].rearrange("p (u c w) -> p u c w", u=2, c=4)
-            nc.vector.tensor_copy(out=dst, in_=src)
+        def on_vector(st, q, a):
+            if st == NS - 1:
+                return q == 1
+            return q == 1 and a == 1 and st % 2 == 1
 
-        def on_vector(st, i, a):
-            if st == NP - 1:
-                return i == 1
-            return i == 1 and a == 1 and st % 2 == 1
-
-        def x_transposes(g, b, a):
-            tau, q = chunk_of[g]
-            row = 256 * CHUNKS[tau]
-            if on_vector(g, b, a):
+        def x_transposes(st, q, a):
+            if on_vector(st, q, a):
                 xt = tpv.tile([P, 4, P], F32, name="xtv", tag="xtv")
             else:
                 xt = tps.tile([P, 4, P], F32, name="xts", tag="xts")
             for aa in range(2):
                 c = 2 * a + aa
                 for u in range(2):
-                    if b == 0 and g >= FIRST_SORTED:
-                        w0 = u * 512 + c * P
-                        src = xd_tiles[g][:, w0 : w0 + P]
+                    if c < SORTED and st >= FIRST_SORTED:
+                        w0 = (u * SORTED + c) * 256 + q * P
+                        src = xd_tiles[st][:, w0 : w0 + P]
                     else:
-                        w0 = (4 * b + c) * row + q * 256
-                        src = xs_tiles[tau][:].bitcast(F32)[:, w0 + u : w0 + 256 : 2]
+                        w0 = c * 512 + q * 256
+                        src = xs_tiles[st][:].bitcast(F32)[:, w0 + u : w0 + 256 : 2]
                     nc.tensor.transpose(xt[:, 2 * aa + u, :], src, ident_f[:])
-            xt_tiles[(g, b, a)] = xt
+            xt_tiles[(st, q, a)] = xt
 
-        def x_copy(st, i, a):
-            xt = xt_tiles[(st, i, a)]
-            if i == 0 and a == 0:
-                xg = xgp.tile([P, 4096], BF16, name="xg", tag="xg", align_bytes=64)
-                xg_tiles[st] = xg
-            xg = xg_tiles[st]
-            h0 = (2 * i + a) * 1024
-            dst = xg[:, h0 : h0 + 1024].bitcast(F32).rearrange("p (a c u) -> p a c u", a=2, u=2)
+        def x_copy(st, q, a):
+            xt = xt_tiles[(st, q, a)]
+            if st not in xg_tiles:
+                xg_tiles[st] = xgp.tile([P, 4096], BF16, name="xg", tag="xg", align_bytes=64)
+            h0 = (2 * q + a) * 1024
+            dst = xg_tiles[st][:, h0 : h0 + 1024].bitcast(F32).rearrange("p (a c u) -> p a c u", a=2, u=2)
             src = xt[:].rearrange("p (a u) c -> p a c u", u=2)
-            if on_vector(st, i, a):
+            if on_vector(st, q, a):
                 nc.vector.tensor_copy(out=dst, in_=src)
             else:
                 nc.scalar.copy(out=dst, in_=src)
@@ -143,69 +134,71 @@ def tile_spatialgather_module_kernel(tc, feats, probs, out):
             xc = xcp.tile([P, 2 * C], U32, name="xc", tag="xc", align_bytes=64)
             xsc = xcp.tile([P, 2 * C], U8, name="xsc", tag="xsc", align_bytes=64)
             xc_tiles[st] = (xc, xsc)
-            for b in range(B) if st == NP - 1 else [0]:
-                w = C if st == NP - 1 else 2 * C
-                nc.vector.quantize_mx(out=xc[:, b * C : b * C + w].bitcast(FP8X4), scales=xsc[:, b * C : b * C + w], in_=xg_tiles[st][:, 4 * b * C : 4 * b * C + 4 * w])
+            w = C if st == NS - 1 else 2 * C
+            for c0 in range(0, 2 * C, w):
+                nc.vector.quantize_mx(
+                    out=xc[:, c0 : c0 + w].bitcast(FP8X4),
+                    scales=xsc[:, c0 : c0 + w],
+                    in_=xg_tiles[st][:, 4 * c0 : 4 * (c0 + w)],
+                )
 
-        def mx_pass(g, b):
-            xc, xsc = xc_tiles[g]
+        def mx_pass(st, q):
+            b = st % 2
+            g = st - b + q
+            xc, xsc = xc_tiles[st]
             w0 = (g % ER) * ESTEP + (1 - b) * P
             nc.tensor.matmul_mx(
                 out=acc[:],
                 lhsT=e_codes[:, w0 : w0 + P].bitcast(FP8X4),
                 lhsT_scale=e_sc[:, w0 : w0 + P],
-                rhs=xc[:, b * C : (b + 1) * C].bitcast(FP8X4),
-                rhs_scale=xsc[:, b * C : (b + 1) * C],
-                start=(g == 0 and b == 0),
-                stop=(g == NP - 1 and b == 1),
+                rhs=xc[:, q * C : (q + 1) * C].bitcast(FP8X4),
+                rhs_scale=xsc[:, q * C : (q + 1) * C],
+                start=(st == 0 and q == 0),
+                stop=(st == NS - 1 and q == 1),
             )
 
-        def e_exp(g):
+        def e_exp(m):
             en = enp.tile([P, 1024], BF16, name="en", tag="en")
-            dst = en[:].rearrange("p (u w e) -> p u w e", u=2, e=2)
-            src = l_sb[:, g * 512 : (g + 2) * 512].rearrange("p (w u e) -> p u w e", u=2, e=2)
             nc.scalar.activation(
-                out=dst, in_=src, func=ACT.Exp, bias=negmax[:, 0:1], scale=1.0, accum_out=rs[:, g // 2 : g // 2 + 1]
+                out=en[:].rearrange("p (u w e) -> p u w e", u=2, e=2),
+                in_=l_sb[:, m * 1024 : (m + 1) * 1024].rearrange("p (w u e) -> p u w e", u=2, e=2),
+                func=ACT.Exp,
+                bias=negmax[:, 0:1],
+                scale=1.0,
+                accum_out=rs[:, m : m + 1],
             )
-            en_tiles[g] = en_tiles[g + 1] = en
+            en_tiles[m] = en
 
-        def e_transposes(g):
-            ew = en_tiles[g][:].bitcast(F32)
-            et = tpe.tile([P, 2, P], F32, name="et", tag="et")
-            for u in range(2):
-                nc.tensor.transpose(et[:, u, :], ew[:, u * 256 + g % 2 * P : u * 256 + g % 2 * P + P], perm_f[:])
-            et_tiles[g] = et
+        def e_transposes(m):
+            ew = en_tiles[m][:].bitcast(F32)
+            et = tpe.tile([P, 4, P], F32, name="et", tag="et")
+            for i in range(4):
+                nc.tensor.transpose(et[:, i, :], ew[:, i * P : (i + 1) * P], perm_f[:])
+            et_tiles[m] = et
 
-        def e_copy(g):
-            eg = egp.tile([P, 512], BF16, name="eg", tag="eg", align_bytes=64)
+        def e_copy(m):
+            eg = egp.tile([P, 1024], BF16, name="eg", tag="eg", align_bytes=64)
             nc.vector.tensor_copy(
-                out=eg[:].bitcast(F32).rearrange("p (r u) -> p r u", u=2), in_=et_tiles[g][:].rearrange("p u r -> p r u")
+                out=eg[:].bitcast(F32).rearrange("p (q r u) -> p q r u", q=2, u=2),
+                in_=et_tiles[m][:].rearrange("p (u q) r -> p q r u", q=2),
             )
-            eg_tiles[g] = eg
+            eg_tiles[m] = eg
 
         def e_quant(g):
             w0 = (g % ER) * ESTEP + 64
+            c0 = g % 2 * 512
             nc.vector.quantize_mx(
-                out=e_codes[:, w0 : w0 + P].bitcast(FP8X4), scales=e_sc[:, w0 : w0 + P], in_=eg_tiles[g][:]
+                out=e_codes[:, w0 : w0 + P].bitcast(FP8X4),
+                scales=e_sc[:, w0 : w0 + P],
+                in_=eg_tiles[g // 2][:, c0 : c0 + 512],
             )
 
         off = 0
         for w in PROB_CHUNKS:
             nc.sync.dma_start(out=l_sb[:, off : off + w], in_=l[:, off : off + w])
             off += w
-        holder = []
-        for tau in range(len(CHUNKS)):
-            same = [t for t in range(tau) if CHUNKS[t] == CHUNKS[tau]]
-            nb = XBUFS[CHUNKS[tau]]
-            holder.append(same[-nb] if len(same) >= nb else -1)
-        loaded = [0]
-
-        def load_more(done):
-            while loaded[0] < len(CHUNKS) and holder[loaded[0]] <= done:
-                load_x(loaded[0])
-                loaded[0] += 1
-
-        load_more(-1)
+        for st in range(XB):
+            load_x(st)
 
         make_identity(nc, ident_f[:])
         nc.gpsimd.tensor_copy(out=perm_f[:, 0:64], in_=ident_f[:, 64:128])
@@ -230,43 +223,44 @@ def tile_spatialgather_module_kernel(tc, feats, probs, out):
             off += w
         nc.vector.tensor_reduce(out=mall[:], in_=mcol[:, 0 : len(PROB_CHUNKS)], axis=AX.X, op=ALU.max)
         nc.vector.tensor_scalar(out=negmax[:], in0=mall[:], scalar1=-1.0, scalar2=None, op0=ALU.mult)
+        e_exp(0)
 
-        for st in range(-2, NP + 3):
+        for st in range(NS + 3):
             for a in range(2):
-                if 0 <= st - 1 < NP and on_vector(st - 1, 1, a):
+                if 0 <= st - 1 < NS and on_vector(st - 1, 1, a):
                     x_copy(st - 1, 1, a)
-            if 0 <= st < NP:
-                for b in range(B):
-                    for a in range(2):
-                        x_transposes(st, b, a)
-                for b in range(B):
-                    for a in range(2):
-                        if not on_vector(st, b, a):
-                            x_copy(st, b, a)
-            if 0 <= st + 2 < NP and st % 2 == 0:
-                e_exp(st + 2)
+            if st < NS:
+                for a in range(2):
+                    for q in range(2):
+                        x_transposes(st, q, a)
+                for a in range(2):
+                    for q in range(2):
+                        if not on_vector(st, q, a):
+                            x_copy(st, q, a)
+                if st % 2 == 0 and st + 2 - 0 < NS:
+                    e_exp(st // 2 + 1)
             if st == 0:
                 e_transposes(0)
-            if 0 <= st < NP:
-                e_copy(st)
-            if 0 <= st - 1 < NP:
+            if st < NS and st % 2 == 0:
+                e_copy(st // 2)
+            if 0 <= st - 1 < NS:
                 x_quant(st - 1)
-            if 0 <= st < NP:
+            if st < NS:
                 e_quant(st)
-            if FIRST_SORTED <= st + 2 < NP and st >= 0:
+            if FIRST_SORTED <= st + 2 < NS:
                 x_prepare(st + 2)
-            if 0 <= st and st + 1 < NP:
-                e_transposes(st + 1)
-            if 0 <= st - 3 < NP:
-                for b in range(B):
-                    mx_pass(st - 3, b)
-            if 0 <= st < NP and chunk_of[st][1] == CHUNKS[chunk_of[st][0]] - 1:
-                load_more(chunk_of[st][0])
-            if st == NP:
+            if st % 2 == 1 and st + 1 < NS:
+                e_transposes((st + 1) // 2)
+            if 0 <= st - 3:
+                for q in range(2):
+                    mx_pass(st - 3, q)
+            if st + XB < NS:
+                load_x(st + XB)
+            if st == NS:
                 nc.vector.tensor_reduce(out=rtot[:], in_=rs[:], axis=AX.X, op=ALU.add)
                 nc.vector.reciprocal(out=rinv[:], in_=rtot[:])
 
-        o_v = o_sb[:].rearrange("p (b t k) -> p b t k", b=B, k=K)
+        o_v = o_sb[:].rearrange("p (a b t k) -> p a b t k", a=2, b=B, k=K)
         for a in range(2):
             nc.vector.tensor_scalar(
                 out=ctx_sb[:, a * 256 : (a + 1) * 256],
@@ -284,7 +278,8 @@ def tile_spatialgather_module_kernel(tc, feats, probs, out):
                 nc.tensor.transpose(ot[:, i, :], ctx_sb[:, t * P : (t + 1) * P], ident_f[:])
             src = ot[:].rearrange("p t (b k) -> p b t k", b=B)
             if a == 0:
-                nc.scalar.copy(out=o_v[:, :, 0:2, :], in_=src)
+                nc.scalar.copy(out=o_v[:, a, :, :, :], in_=src)
             else:
-                nc.vector.tensor_copy(out=o_v[:, :, 2:4, :], in_=src)
-        nc.sync.dma_start(out=o, in_=o_sb[:].rearrange("p (g k) -> p g k", k=K))
+                nc.vector.tensor_copy(out=o_v[:, a, :, :, :], in_=src)
+            for b in range(B):
+                nc.sync.dma_start(out=o[:, b, 2 * a : 2 * a + 2, :], in_=o_v[:, a, b, :, :])

@@ -34,7 +34,7 @@ def tile_spatialgather_module_kernel(tc, feats, probs, out):
     nc = tc.nc
     x = feats.rearrange("b c h w -> b c (h w)")
     l = probs.rearrange("b k h w -> (b k) (h w)")
-    o = out.rearrange("b (t p) k o -> p b t (k o)", p=P)
+    o = out.rearrange("b (t p) k o -> p (b t) (k o)", p=P)
 
     with ExitStack() as ctx:
         const = ctx.enter_context(tc.tile_pool(name="const", bufs=1))
@@ -44,7 +44,7 @@ def tile_spatialgather_module_kernel(tc, feats, probs, out):
         xcp = ctx.enter_context(tc.tile_pool(name="xcp", bufs=XCB))
         jkp = ctx.enter_context(tc.tile_pool(name="jkp", bufs=2))
         enp = ctx.enter_context(tc.tile_pool(name="enp", bufs=3))
-        egp = ctx.enter_context(tc.tile_pool(name="egp", bufs=2))
+        egp = ctx.enter_context(tc.tile_pool(name="egp", bufs=3))
         accp = ctx.enter_context(tc.psum_pool(name="accp", bufs=1))
         tps = ctx.enter_context(tc.psum_pool(name="tps", bufs=4))
         tpv = ctx.enter_context(tc.psum_pool(name="tpv", bufs=2))
@@ -170,27 +170,26 @@ def tile_spatialgather_module_kernel(tc, feats, probs, out):
             en_tiles[m] = en
 
         def e_transposes(m):
-            ew = en_tiles[m][:].bitcast(F32)
-            et = tpe.tile([P, 4, P], F32, name="et", tag="et")
-            for i in range(4):
-                nc.tensor.transpose(et[:, i, :], ew[:, i * P : (i + 1) * P], perm_f[:])
+            ew = en_tiles[m // 2][:].bitcast(F32)
+            et = tpe.tile([P, 2, P], F32, name="et", tag="et")
+            for u in range(2):
+                w0 = u * 256 + m % 2 * P
+                nc.tensor.transpose(et[:, u, :], ew[:, w0 : w0 + P], perm_f[:])
             et_tiles[m] = et
 
         def e_copy(m):
-            eg = egp.tile([P, 1024], BF16, name="eg", tag="eg", align_bytes=64)
+            eg = egp.tile([P, 512], BF16, name="eg", tag="eg", align_bytes=64)
             nc.vector.tensor_copy(
-                out=eg[:].bitcast(F32).rearrange("p (q r u) -> p q r u", q=2, u=2),
-                in_=et_tiles[m][:].rearrange("p (u q) r -> p q r u", q=2),
+                out=eg[:].bitcast(F32).rearrange("p (r u) -> p r u", u=2), in_=et_tiles[m][:].rearrange("p u r -> p r u")
             )
             eg_tiles[m] = eg
 
         def e_quant(g):
             w0 = (g % ER) * ESTEP + 64
-            c0 = g % 2 * 512
             nc.vector.quantize_mx(
                 out=e_codes[:, w0 : w0 + P].bitcast(FP8X4),
                 scales=e_sc[:, w0 : w0 + P],
-                in_=eg_tiles[g // 2][:, c0 : c0 + 512],
+                in_=eg_tiles[g][:],
             )
 
         off = 0
@@ -241,16 +240,16 @@ def tile_spatialgather_module_kernel(tc, feats, probs, out):
                     e_exp(st // 2 + 1)
             if st == 0:
                 e_transposes(0)
-            if st < NS and st % 2 == 0:
-                e_copy(st // 2)
+            if st < NS:
+                e_copy(st)
             if 0 <= st - 1 < NS:
                 x_quant(st - 1)
             if st < NS:
                 e_quant(st)
             if FIRST_SORTED <= st + 2 < NS:
                 x_prepare(st + 2)
-            if st % 2 == 1 and st + 1 < NS:
-                e_transposes((st + 1) // 2)
+            if st + 1 < NS:
+                e_transposes(st + 1)
             if 0 <= st - 3:
                 for q in range(2):
                     mx_pass(st - 3, q)
@@ -260,7 +259,7 @@ def tile_spatialgather_module_kernel(tc, feats, probs, out):
                 nc.vector.tensor_reduce(out=rtot[:], in_=rs[:], axis=AX.X, op=ALU.add)
                 nc.vector.reciprocal(out=rinv[:], in_=rtot[:])
 
-        o_v = o_sb[:].rearrange("p (a b t k) -> p a b t k", a=2, b=B, k=K)
+        o_v = o_sb[:].rearrange("p (b t k) -> p b t k", b=B, k=K)
         for a in range(2):
             nc.vector.tensor_scalar(
                 out=ctx_sb[:, a * 256 : (a + 1) * 256],
@@ -278,8 +277,7 @@ def tile_spatialgather_module_kernel(tc, feats, probs, out):
                 nc.tensor.transpose(ot[:, i, :], ctx_sb[:, t * P : (t + 1) * P], ident_f[:])
             src = ot[:].rearrange("p t (b k) -> p b t k", b=B)
             if a == 0:
-                nc.scalar.copy(out=o_v[:, a, :, :, :], in_=src)
+                nc.scalar.copy(out=o_v[:, :, 0:2, :], in_=src)
             else:
-                nc.vector.tensor_copy(out=o_v[:, a, :, :, :], in_=src)
-            for b in range(B):
-                nc.sync.dma_start(out=o[:, b, 2 * a : 2 * a + 2, :], in_=o_v[:, a, b, :, :])
+                nc.vector.tensor_copy(out=o_v[:, :, 2:4, :], in_=src)
+        nc.sync.dma_start(out=o, in_=o_sb[:].rearrange("p (g k) -> p g k", k=K))

from contextlib import ExitStack

import concourse.mybir as mybir
from concourse.masks import make_identity

F32 = mybir.dt.float32
BF16 = mybir.dt.bfloat16
U32 = mybir.dt.uint32
U8 = mybir.dt.uint8
I32 = mybir.dt.int32
FP8X4 = mybir.dt.float8_e4m3fn_x4
ALU = mybir.AluOpType
ACT = mybir.ActivationFunctionType
AX = mybir.AxisListType

P = 128
B, C, K, N = 2, 512, 64, 16384
FLOPS = 2 * B * K * C * N

NP = N // 512
NS = NP
PROB_CHUNKS = (2048, 2048, 2048, 2048, 2048, 2048, 2048, 1024, 1024)
XB = 13
SPLIT_LOADS = 8
ESTEP = 192
ER = 8
XGB = 3
XCB = 4
SORTED = 2
FIRST_SORTED = 4


def tile_spatialgather_module_kernel(tc, feats, probs, out):
    nc = tc.nc
    x = feats.rearrange("b c h w -> b c (h w)")
    l = probs.rearrange("b k h w -> (b k) (h w)")
    o = out.rearrange("b (t p) k o -> p (b t) (k o)", p=P)

    with ExitStack() as ctx:
        const = ctx.enter_context(tc.tile_pool(name="const", bufs=1))
        xsp = ctx.enter_context(tc.tile_pool(name="xsp", bufs=XB))
        xdp = ctx.enter_context(tc.tile_pool(name="xdp", bufs=2))
        xgp = ctx.enter_context(tc.tile_pool(name="xgp", bufs=XGB))
        xcp = ctx.enter_context(tc.tile_pool(name="xcp", bufs=XCB))
        jkp = ctx.enter_context(tc.tile_pool(name="jkp", bufs=2))
        enp = ctx.enter_context(tc.tile_pool(name="enp", bufs=3))
        egp = ctx.enter_context(tc.tile_pool(name="egp", bufs=3))
        accp = ctx.enter_context(tc.psum_pool(name="accp", bufs=1))
        tps = ctx.enter_context(tc.psum_pool(name="tps", bufs=4))
        tpv = ctx.enter_context(tc.psum_pool(name="tpv", bufs=2))
        tpe = ctx.enter_context(tc.psum_pool(name="tpe", bufs=1))
        ctx.enter_context(tc.manual_schedule())

        ident_f = const.tile([P, P], F32, name="ident_f")
        perm_f = const.tile([P, P], F32, name="perm_f")
        l_sb = const.tile([P, N], BF16, name="l_sb")
        e_codes = const.tile([P, ER * ESTEP + 64], U32, name="e_codes", align_bytes=64)
        e_sc = const.tile([P, ER * ESTEP + 64], U8, name="e_sc", align_bytes=64)
        mcol = const.tile([P, 16], F32, name="mcol")
        mall = const.tile([P, 1], F32, name="mall")
        negmax = const.tile([P, 1], F32, name="negmax")
        rs = const.tile([P, NP // 2], F32, name="rs")
        rtot = const.tile([P, 1], F32, name="rtot")
        rinv = const.tile([P, 1], F32, name="rinv")
        scr0 = const.tile([P, 1], F32, name="scr0")
        scr1 = const.tile([P, 1], F32, name="scr1")
        ctx_sb = const.tile([P, C], F32, name="ctx_sb")
        o_sb = const.tile([P, C], F32, name="o_sb")
        acc = accp.tile([P, C], F32, name="acc")

        xs_tiles = {}
        xd_tiles = {}
        xt_tiles = {}
        xg_tiles = {}
        xc_tiles = {}
        en_tiles = {}
        et_tiles = {}
        eg_tiles = {}

        def load_x(st):
            m, b = st // 2, st % 2
            xs = xsp.tile([P, 4096], BF16, name="xs", tag="xs")
            dst = xs[:].rearrange("p (c n) -> p c n", c=4)
            src = x[b, :, m * 1024 : (m + 1) * 1024].rearrange("(c p) n -> p c n", p=P)
            w = 2 if st < SPLIT_LOADS else 4
            for c in range(0, 4, w):
                nc.sync.dma_start(out=dst[:, c : c + w, :], in_=src[:, c : c + w, :])
            xs_tiles[st] = xs

        def x_prepare(st):
            xd = xdp.tile([P, 512 * SORTED], F32, name="xd", tag="xd")
            src = xs_tiles[st][:].bitcast(F32)[:, 0 : 512 * SORTED]
            nc.vector.tensor_copy(
                out=xd[:].rearrange("p (u c w) -> p u c w", u=2, c=SORTED),
                in_=src.rearrange("p (c w u) -> p u c w", c=SORTED, u=2),
            )
            xd_tiles[st] = xd

        def on_vector(st, q, a):
            if st == NS - 1:
                return q == 1
            return q == 1 and a == 1 and st % 2 == 1

        def x_transposes(st, q, a):
            if on_vector(st, q, a):
                xt = tpv.tile([P, 4, P], F32, name="xtv", tag="xtv")
            else:
                xt = tps.tile([P, 4, P], F32, name="xts", tag="xts")
            for aa in range(2):
                c = 2 * a + aa
                for u in range(2):
                    if c < SORTED and st >= FIRST_SORTED:
                        w0 = (u * SORTED + c) * 256 + q * P
                        src = xd_tiles[st][:, w0 : w0 + P]
                    else:
                        w0 = c * 512 + q * 256
                        src = xs_tiles[st][:].bitcast(F32)[:, w0 + u : w0 + 256 : 2]
                    nc.tensor.transpose(xt[:, 2 * aa + u, :], src, ident_f[:])
            xt_tiles[(st, q, a)] = xt

        def x_copy(st, q, a):
            xt = xt_tiles[(st, q, a)]
            if st not in xg_tiles:
                xg_tiles[st] = xgp.tile([P, 4096], BF16, name="xg", tag="xg", align_bytes=64)
            h0 = (2 * q + a) * 1024
            dst = xg_tiles[st][:, h0 : h0 + 1024].bitcast(F32).rearrange("p (a c u) -> p a c u", a=2, u=2)
            src = xt[:].rearrange("p (a u) c -> p a c u", u=2)
            if on_vector(st, q, a):
                nc.vector.tensor_copy(out=dst, in_=src)
            else:
                nc.scalar.copy(out=dst, in_=src)

        def x_quant(st):
            xc = xcp.tile([P, 2 * C], U32, name="xc", tag="xc", align_bytes=64)
            xsc = xcp.tile([P, 2 * C], U8, name="xsc", tag="xsc", align_bytes=64)
            xc_tiles[st] = (xc, xsc)
            w = C if st == NS - 1 else 2 * C
            for c0 in range(0, 2 * C, w):
                nc.vector.quantize_mx(
                    out=xc[:, c0 : c0 + w].bitcast(FP8X4),
                    scales=xsc[:, c0 : c0 + w],
                    in_=xg_tiles[st][:, 4 * c0 : 4 * (c0 + w)],
                )

        def mx_pass(st, q):
            b = st % 2
            g = st - b + q
            xc, xsc = xc_tiles[st]
            w0 = (g % ER) * ESTEP + (1 - b) * P
            nc.tensor.matmul_mx(
                out=acc[:],
                lhsT=e_codes[:, w0 : w0 + P].bitcast(FP8X4),
                lhsT_scale=e_sc[:, w0 : w0 + P],
                rhs=xc[:, q * C : (q + 1) * C].bitcast(FP8X4),
                rhs_scale=xsc[:, q * C : (q + 1) * C],
                start=(st == 0 and q == 0),
                stop=(st == NS - 1 and q == 1),
            )

        def e_exp(m):
            en = enp.tile([P, 1024], BF16, name="en", tag="en")
            nc.scalar.activation(
                out=en[:].rearrange("p (u w e) -> p u w e", u=2, e=2),
                in_=l_sb[:, m * 1024 : (m + 1) * 1024].rearrange("p (w u e) -> p u w e", u=2, e=2),
                func=ACT.Exp,
                bias=negmax[:, 0:1],
                scale=1.0,
                accum_out=rs[:, m : m + 1],
            )
            en_tiles[m] = en

        def e_transposes(m):
            ew = en_tiles[m // 2][:].bitcast(F32)
            et = tpe.tile([P, 2, P], F32, name="et", tag="et")
            for u in range(2):
                w0 = u * 256 + m % 2 * P
                nc.tensor.transpose(et[:, u, :], ew[:, w0 : w0 + P], perm_f[:])
            et_tiles[m] = et

        def e_copy(m):
            eg = egp.tile([P, 512], BF16, name="eg", tag="eg", align_bytes=64)
            nc.vector.tensor_copy(
                out=eg[:].bitcast(F32).rearrange("p (r u) -> p r u", u=2), in_=et_tiles[m][:].rearrange("p u r -> p r u")
            )
            eg_tiles[m] = eg

        def e_quant(g):
            w0 = (g % ER) * ESTEP + 64
            nc.vector.quantize_mx(
                out=e_codes[:, w0 : w0 + P].bitcast(FP8X4),
                scales=e_sc[:, w0 : w0 + P],
                in_=eg_tiles[g][:],
            )

        off = 0
        for w in PROB_CHUNKS:
            nc.sync.dma_start(out=l_sb[:, off : off + w], in_=l[:, off : off + w])
            off += w
        for st in range(XB):
            load_x(st)

        make_identity(nc, ident_f[:])
        nc.gpsimd.tensor_copy(out=perm_f[:, 0:64], in_=ident_f[:, 64:128])
        nc.gpsimd.tensor_copy(out=perm_f[:, 64:128], in_=ident_f[:, 0:64])
        nc.vector.memset(scr0[:], 0.0)
        nc.vector.memset(e_codes[:].bitcast(I32), 0)
        nc.vector.memset(e_sc[:].bitcast(I32), 0)
        nc.scalar.activation(out=scr1[:], in_=scr0[:], func=ACT.Exp)

        off = 0
        for i, w in enumerate(PROB_CHUNKS):
            junk = jkp.tile([P, w], BF16, name="junk", tag="junk")
            nc.vector.tensor_scalar(
                out=junk[:],
                in0=l_sb[:, off : off + w],
                scalar1=0.0,
                scalar2=None,
                op0=ALU.add,
                op1=ALU.max,
                accum_out=mcol[:, i : i + 1],
            )
            off += w
        nc.vector.tensor_reduce(out=mall[:], in_=mcol[:, 0 : len(PROB_CHUNKS)], axis=AX.X, op=ALU.max)
        nc.vector.tensor_scalar(out=negmax[:], in0=mall[:], scalar1=-1.0, scalar2=None, op0=ALU.mult)
        e_exp(0)

        for st in range(NS + 3):
            for a in range(2):
                if 0 <= st - 1 < NS and on_vector(st - 1, 1, a):
                    x_copy(st - 1, 1, a)
            if st < NS:
                for a in range(2):
                    for q in range(2):
                        x_transposes(st, q, a)
                for a in range(2):
                    for q in range(2):
                        if not on_vector(st, q, a):
                            x_copy(st, q, a)
                if st % 2 == 0 and st + 2 - 0 < NS:
                    e_exp(st // 2 + 1)
            if st == 0:
                e_transposes(0)
            if st < NS:
                e_copy(st)
            if 0 <= st - 1 < NS:
                x_quant(st - 1)
            if st < NS:
                e_quant(st)
            if FIRST_SORTED <= st + 2 < NS:
                x_prepare(st + 2)
            if st + 1 < NS:
                e_transposes(st + 1)
            if 0 <= st - 3:
                for q in range(2):
                    mx_pass(st - 3, q)
            if st + XB < NS:
                load_x(st + XB)
            if st == NS:
                nc.vector.tensor_reduce(out=rtot[:], in_=rs[:], axis=AX.X, op=ALU.add)
                nc.vector.reciprocal(out=rinv[:], in_=rtot[:])

        o_v = o_sb[:].rearrange("p (b t k) -> p b t k", b=B, k=K)
        for a in range(2):
            nc.vector.tensor_scalar(
                out=ctx_sb[:, a * 256 : (a + 1) * 256],
                in0=acc[:, a * 256 : (a + 1) * 256],
                scalar1=rinv[:, 0:1],
                scalar2=None,
                op0=ALU.mult,
            )
            if a == 0:
                ot = tpv.tile([P, 2, P], F32, name="otv", tag="xtv")
            else:
                ot = tps.tile([P, 2, P], F32, name="ots", tag="xts")
            for i in range(2):
                t = 2 * a + i
                nc.tensor.transpose(ot[:, i, :], ctx_sb[:, t * P : (t + 1) * P], ident_f[:])
            src = ot[:].rearrange("p t (b k) -> p b t k", b=B)
            if a == 0:
                nc.scalar.copy(out=o_v[:, :, 0:2, :], in_=src)
            else:
                nc.vector.tensor_copy(out=o_v[:, :, 2:4, :], in_=src)
        nc.sync.dma_start(out=o, in_=o_sb[:].rearrange("p (g k) -> p g k", k=K))
